import numpy as np
import ml_dtypes


def mxq(x, axis, fmt="e4m3"):
    dtype, down = {"e4m3": (ml_dtypes.float8_e4m3fn, 7), "e5m2": (ml_dtypes.float8_e5m2, 14)}[fmt]
    v = np.moveaxis(np.asarray(x, np.float32).astype(ml_dtypes.bfloat16).astype(np.float64), axis, -1)
    blocks = v.reshape(v.shape[:-1] + (-1, 32))
    amax = np.abs(blocks).max(-1, keepdims=True)
    byte = np.maximum(np.where(amax > 0, np.frexp(amax)[1] - 1 + 127, 0) - down, 1)
    scale = np.exp2(byte - 127.0)
    codes = (blocks / scale).astype(np.float32).astype(dtype).astype(np.float64)
    return np.moveaxis((codes * scale).reshape(v.shape), -1, axis)


WIDE = False


def mx_kscale(k):
    if not WIDE:
        return np.ones(k)
    levels = np.array([10, -10, 5, -5, 0])
    a = np.random.permutation(np.resize(levels, k // 512 * 4)).reshape(k // 512, 4)
    idx = np.arange(k)
    return np.exp2(a[idx // 512, idx % 128 // 32])


BF16 = ml_dtypes.bfloat16


def bf(x):
    return np.asarray(x, np.float32).astype(BF16)


def f64(x):
    return np.asarray(x).astype(np.float64)


E2M1 = np.array([0.0, 0.5, 1.0, 1.5, 2.0, 3.0, 4.0, 6.0, -0.0, -0.5, -1.0, -1.5, -2.0, -3.0, -4.0, -6.0])


def pack_weight(w, fmt):
    k, n = w.shape
    w = f64(bf(w)).reshape(k // 32, 32, n)
    amax = np.abs(w).max(1)
    if fmt == "e4m3":
        byte = np.frexp(amax)[1] - 1 + 127 - 7
    else:
        mant, ex = np.frexp(amax / 6.0)
        byte = np.where(mant > 0.5, ex, ex - 1) + 127
    byte = np.clip(np.where(amax > 0, byte, 1), 1, 254)
    scaled = (w * np.exp2(127.0 - byte)[:, None, :]).reshape(k, n).astype(np.float32)
    by_word = np.ascontiguousarray(scaled.reshape(k // 512, 128, 4, n).transpose(0, 1, 3, 2))
    if fmt == "e4m3":
        words = by_word.astype(ml_dtypes.float8_e4m3fn).view(np.uint8)
    else:
        c = by_word.astype(ml_dtypes.float4_e2m1fn).view(np.uint8) & 0xF
        words = c[..., 0::2] | (c[..., 1::2] << 4)
    return np.ascontiguousarray(words), np.ascontiguousarray(byte.astype(np.uint8).reshape(k // 512, 16, n))


def unpack_weight(words, scales, fmt):
    g, p, n, _ = words.shape
    if fmt == "e4m3":
        vals = np.ascontiguousarray(words).view(ml_dtypes.float8_e4m3fn).astype(np.float64)
    else:
        nib = np.empty((g, p, n, 4), np.uint8)
        nib[..., 0::2] = words & 0xF
        nib[..., 1::2] = words >> 4
        vals = E2M1[nib]
    vals = vals * np.repeat(np.exp2(scales.astype(np.float64) - 127.0), 8, axis=1)[..., None]
    return vals.transpose(0, 1, 3, 2).reshape(g * 512, n)


B, I, H = 1024, 512, 512
FMT = "e4m3"


def sigmoid(v):
    return 1.0 / (1.0 + np.exp(-v))


def setup_inputs():
    s = mx_kscale(I)
    x = bf(np.random.standard_normal((B, I)) * s)
    h_prev = bf(np.random.standard_normal((B, H)))
    c_prev = bf(np.random.standard_normal((B, H)))
    w_ih = np.random.standard_normal((4 * H, I)) * 1.0 / np.sqrt(I) / s[None, :]
    w_ih_words, w_ih_scales = pack_weight(np.ascontiguousarray(w_ih.T), FMT)
    w_hh = bf(np.random.standard_normal((4 * H, H)) * 1.0 / np.sqrt(H))
    bias_ih = bf(np.random.standard_normal(4 * H) * 0.5)
    bias_hh = bf(np.random.standard_normal(4 * H) * 0.5)
    return {"x": x,
            "h_prev": h_prev,
            "c_prev": c_prev,
            "w_ih_words": w_ih_words,
            "w_ih_scales": w_ih_scales,
            "w_hh": w_hh,
            "bias_ih": bias_ih,
            "bias_hh": bias_hh}


def reference(x, h_prev, c_prev, w_ih_words, w_ih_scales, w_hh, bias_ih, bias_hh):
    gates = (mxq(f64(x), 1, "e4m3") @ unpack_weight(w_ih_words, w_ih_scales, FMT)) + f64(bias_ih) + f64(h_prev) @ f64(w_hh).T + f64(bias_hh)
    i_g, f_g, g_g, o_g = np.split(gates, 4, axis=1)
    i_g = sigmoid(i_g)
    f_g = sigmoid(f_g)
    g_g = np.tanh(g_g)
    o_g = sigmoid(o_g)
    c_new = f_g * f64(c_prev) + i_g * g_g
    h_new = o_g * np.tanh(c_new)
    return (h_new, c_new)

@@ -1,0 +1,385 @@
+from contextlib import ExitStack
+
+import concourse.mybir as mybir
+from concourse.masks import make_identity
+
+BF16 = mybir.dt.bfloat16
+F32 = mybir.dt.float32
+I32 = mybir.dt.int32
+U32 = mybir.dt.uint32
+U8 = mybir.dt.uint8
+FP8X4 = mybir.dt.float8_e4m3fn_x4
+ADD = mybir.AluOpType.add
+MULT = mybir.AluOpType.mult
+SIGMOID = mybir.ActivationFunctionType.Sigmoid
+TANH = mybir.ActivationFunctionType.Tanh
+
+P = 128
+BATCH = 1024
+FEAT = 512
+N_GATES = 4
+GATE_COLS = N_GATES * FEAT
+TILES = BATCH // P
+K_CHUNKS = FEAT // P
+WORD_CHUNKS = FEAT // 2 // P
+PAIR = 2
+PAIRS = TILES // PAIR
+ROW_TILES = FEAT // P
+BLOCKS = PAIRS * N_GATES
+GROUPS = BLOCKS * PAIR
+WARM_UPS = 4
+MX_LEAD = 8
+
+FLOPS = 2 * BATCH * FEAT * GATE_COLS * 2
+
+
+def tile_int8lstmcell_kernel(
+    tc, x, h_prev, c_prev, w_ih_words, w_ih_scales, w_hh, bias_ih, bias_hh, out_0, out_1
+):
+    nc = tc.nc
+    with ExitStack() as stack:
+        keep = stack.enter_context(tc.tile_pool(name="keep", bufs=1))
+        psum = stack.enter_context(tc.psum_pool(name="psum", bufs=8))
+        stack.enter_context(tc.manual_schedule())
+
+        x_view = x.rearrange("(p b) k -> p b k", b=TILES)
+        h_view = h_prev.rearrange("(p b) k -> p b k", b=TILES)
+        c_view = c_prev.rearrange("(p b) k -> p b k", b=TILES)
+        h_new_view = out_0.rearrange("(p b) n -> p b n", b=TILES)
+        c_new_view = out_1.rearrange("(p b) n -> p b n", b=TILES)
+        w_hh_view = w_hh.rearrange("(j p) k -> p j k", p=P)
+        words_view = w_ih_words[0].rearrange("p n t -> p (n t)")
+
+        x_sb = keep.tile([P, TILES, FEAT], BF16)
+        h_sb = keep.tile([P, TILES, FEAT], BF16)
+        c_sb = keep.tile([P, TILES, FEAT], BF16)
+        w_sb = keep.tile([P, N_GATES * ROW_TILES, FEAT], BF16)
+        w_words = keep.tile([P, GATE_COLS], U32, align_bytes=64)
+        w_plane = keep.tile([P, GATE_COLS], U8, align_bytes=64)
+        bias_rows = keep.tile([P, GATE_COLS], BF16)
+        bias_all = keep.tile([P, GATE_COLS], F32)
+        ones = keep.tile([P, P], BF16)
+        zeros = keep.tile([P, FEAT], BF16)
+        ident_f32 = keep.tile([P, P], F32)
+        warm = keep.tile([P, 1], F32)
+        x_grouped = keep.tile([P, BATCH * 4], BF16, align_bytes=64)
+        x_codes = keep.tile([P, BATCH], U32, align_bytes=64)
+        x_plane = keep.tile([P, BATCH], U8, align_bytes=64)
+        h_t = keep.tile([P, WORD_CHUNKS, BATCH], F32)
+        w_t = keep.tile([P, WORD_CHUNKS, GATE_COLS], F32)
+        h_t_halves = h_t[:].rearrange("p j r -> p (j r)").bitcast(BF16).rearrange("p (j r e) -> p j r e", j=WORD_CHUNKS, e=2)
+        w_t_halves = w_t[:].rearrange("p j r -> p (j r)").bitcast(BF16).rearrange("p (j r e) -> p j r e", j=WORD_CHUNKS, e=2)
+        gates = keep.tile([P, TILES, GATE_COLS], F32)
+        c_new = keep.tile([P, TILES, FEAT], F32)
+        h_new = keep.tile([P, TILES, FEAT], F32)
+
+        def gate(b, g, lo=0, hi=FEAT):
+            return gates[:, b, g * FEAT + lo : g * FEAT + hi]
+
+        nc.vector.memset(ones[:], 1.0)
+        nc.gpsimd.memset(zeros[:], 0.0)
+        nc.vector.memset(bias_rows[:].bitcast(I32), 0)
+        nc.vector.memset(w_plane[:].bitcast(I32), 0)
+        nc.vector.memset(warm[:], 0.0)
+        make_identity(nc, ident_f32[:])
+        nc.scalar.activation(out=warm[:], in_=warm[:], func=SIGMOID)
+
+        def load_pair(dst, src, q):
+            nc.sync.dma_start(out=dst[:, q * PAIR : (q + 1) * PAIR, :], in_=src[:, q * PAIR : (q + 1) * PAIR, :])
+
+        def load_w_hh(jj):
+            row_tiles = slice(jj * PAIR, (jj + 1) * PAIR)
+            nc.sync.dma_start(out=w_sb[:, row_tiles, :], in_=w_hh_view[:, row_tiles, :])
+
+        def load_words(g):
+            nc.sync.dma_start(
+                out=w_words[:, g * FEAT : (g + 1) * FEAT].bitcast(I32),
+                in_=words_view[:, g * FEAT * 4 : (g + 1) * FEAT * 4].bitcast(I32),
+            )
+
+        load_pair(h_sb, h_view, 0)
+        nc.sync.dma_start(out=bias_rows[0:1, :], in_=bias_ih.rearrange("(o n) -> o n", o=1))
+        nc.sync.dma_start(out=bias_rows[1:2, :], in_=bias_hh.rearrange("(o n) -> o n", o=1))
+        load_w_hh(0)
+        load_w_hh(1)
+        load_w_hh(2)
+        load_pair(x_sb, x_view, 0)
+        load_w_hh(3)
+        for s in range(4):
+            nc.sync.dma_start(
+                out=w_plane[32 * s : 32 * s + 4, :].bitcast(I32),
+                in_=w_ih_scales[0, 4 * s : 4 * s + 4, :].bitcast(I32),
+            )
+        load_words(0)
+        load_words(1)
+        load_w_hh(4)
+        load_pair(x_sb, x_view, 1)
+        load_w_hh(5)
+        load_words(2)
+        load_w_hh(6)
+        load_w_hh(7)
+        load_words(3)
+        for q in range(PAIRS):
+            load_pair(c_sb, c_view, q)
+            if q + 1 < PAIRS:
+                load_pair(h_sb, h_view, q + 1)
+            if q + 2 < PAIRS:
+                load_pair(x_sb, x_view, q + 2)
+
+        grouped_words = x_grouped[:].bitcast(F32).rearrange("p (b r u) -> p b r u", b=TILES, u=2)
+
+        def x_transposes(x_ps, q):
+            return [
+                (x_ps[:, t, u, :], x_sb[:, q * PAIR + t, :].bitcast(F32)[:, u : FEAT // 2 : 2], ident_f32[:])
+                for t in range(PAIR)
+                for u in range(2)
+            ]
+
+        def x_copy(x_ps, q):
+            nc.scalar.copy(
+                out=grouped_words[:, q * PAIR : (q + 1) * PAIR, :, :], in_=x_ps[:].rearrange("p t u r -> p t r u")
+            )
+
+        def x_quantise(q):
+            rows = slice(q * PAIR * P, (q + 1) * PAIR * P)
+            nc.vector.quantize_mx(
+                out=x_codes[:, rows].bitcast(FP8X4),
+                scales=x_plane[:, rows],
+                in_=x_grouped[:, q * PAIR * P * 4 : (q + 1) * PAIR * P * 4],
+            )
+
+        def mx_pass(b, g):
+            rows = slice(b * P, (b + 1) * P)
+            cols = slice(g * FEAT, (g + 1) * FEAT)
+            mx_ps = psum.tile([P, FEAT], F32, tag="bank")
+            nc.tensor.matmul_mx(
+                out=mx_ps[:],
+                lhsT=x_codes[:, rows].bitcast(FP8X4),
+                lhsT_scale=x_plane[:, rows],
+                rhs=w_words[:, cols].bitcast(FP8X4),
+                rhs_scale=w_plane[:, cols],
+                start=True,
+                stop=True,
+            )
+            return mx_ps
+
+        begun = set()
+
+        def fetch(sums_ps, b, g, lo=0, hi=FEAT):
+            complete = (b, g) in begun
+            other = gate(b, g, lo, hi) if complete else bias_all[:, g * FEAT + lo : g * FEAT + hi]
+            nc.vector.tensor_tensor(out=gate(b, g, lo, hi), in0=sums_ps[:], in1=other, op=ADD)
+            if hi == FEAT:
+                begun.add((b, g))
+            return complete
+
+        def w_flip(jj):
+            return ([w_sb[:, jj * PAIR + i, :] for i in range(PAIR)], w_t[:, :, jj * PAIR * P : (jj + 1) * PAIR * P])
+
+        def h_flip(q):
+            return ([h_sb[:, q * PAIR + i, :] for i in range(PAIR)], h_t[:, :, q * PAIR * P : (q + 1) * PAIR * P])
+
+        def flip_transposes(flip_ps, flip):
+            return [
+                (flip_ps[:, j, i, :], flip[0][i].bitcast(F32)[:, j * P : (j + 1) * P], ident_f32[:])
+                for i in range(PAIR)
+                for j in range(WORD_CHUNKS)
+            ]
+
+        def flip_copy(flip_ps, flip):
+            nc.scalar.copy(out=flip[1], in_=flip_ps[:].rearrange("p j i r -> p j (i r)"))
+
+        def plain_matmuls(sums, b, g, lo, hi, riders):
+            share = -(-len(riders) // (K_CHUNKS - 1))
+            for kc in range(K_CHUNKS):
+                nc.tensor.matmul(
+                    out=sums,
+                    lhsT=h_t_halves[:, kc // 2, b * P : (b + 1) * P, kc % 2],
+                    rhs=w_t_halves[:, kc // 2, g * FEAT + lo : g * FEAT + hi, kc % 2],
+                    start=(kc == 0),
+                    stop=(kc == K_CHUNKS - 1),
+                )
+                if kc > 0 or len(riders) > 2 * share:
+                    first = (kc - 1 if len(riders) <= 2 * share else kc) * share
+                    for out, in_, identity in riders[first : first + share]:
+                        nc.tensor.transpose(out, in_, identity)
+
+        def plain_group(b, g, riders):
+            pl_ps = psum.tile([P, FEAT], F32, tag="bank")
+            plain_matmuls(pl_ps[:], b, g, 0, FEAT, riders)
+            return pl_ps
+
+        def activate(b, g, lo=0, hi=FEAT):
+            nc.scalar.activation(out=gate(b, g, lo, hi), in_=gate(b, g, lo, hi), func=(TANH if g == 2 else SIGMOID))
+
+        def f_times_c(cell, b):
+            cell.tensor_tensor(out=gate(b, 1), in0=gate(b, 1), in1=c_sb[:, b, :], op=MULT)
+
+        def i_times_g(cell, b):
+            cell.tensor_tensor(out=gate(b, 0), in0=gate(b, 0), in1=gate(b, 2), op=MULT)
+
+        def c_sum(cell, b):
+            cell.tensor_tensor(out=c_new[:, b, :], in0=gate(b, 1), in1=gate(b, 0), op=ADD)
+            nc.sync.dma_start(out=c_new_view[:, b, :], in_=c_new[:, b, :])
+
+        def tanh_c_new(b):
+            nc.scalar.activation(out=gate(b, 2), in_=c_new[:, b, :], func=TANH)
+
+        def h_store(b, lo=0, hi=FEAT):
+            nc.sync.dma_start(out=h_new_view[:, b, lo:hi], in_=h_new[:, b, lo:hi])
+
+        def h_product(cell, b, lo=0, hi=FEAT, store_now=True):
+            cell.tensor_tensor(out=h_new[:, b, lo:hi], in0=gate(b, 3, lo, hi), in1=gate(b, 2, lo, hi), op=MULT)
+            if store_now:
+                h_store(b, lo, hi)
+
+        def flip_now(flip):
+            flip_ps = psum.tile([P, WORD_CHUNKS, PAIR, P], F32, tag="bank")
+            for out, in_, identity in flip_transposes(flip_ps, flip):
+                nc.tensor.transpose(out, in_, identity)
+            flip_copy(flip_ps, flip)
+
+        def spread_biases(g, copy):
+            cols = slice(g * FEAT, (g + 1) * FEAT)
+            bias_ps = psum.tile([P, FEAT], F32, tag="bank")
+            nc.tensor.matmul(out=bias_ps[:], lhsT=ones[:], rhs=bias_rows[:, cols], start=True, stop=True)
+            copy(out=bias_all[:, cols], in_=bias_ps[:])
+
+        warm_ps = psum.tile([P, FEAT], F32, tag="bank")
+        for i in range(WARM_UPS):
+            nc.tensor.matmul(out=warm_ps[:], lhsT=ones[:], rhs=zeros[:], start=True, stop=True)
+        flip_now(h_flip(0))
+        spread_biases(0, nc.vector.tensor_copy)
+        flip_now(w_flip(0))
+        spread_biases(1, nc.vector.tensor_copy)
+        flip_now(w_flip(1))
+        spread_biases(2, nc.vector.tensor_copy)
+
+        block_order = []
+        for q in range(PAIRS):
+            block_order.extend([(q, g) for g in range(N_GATES - 1)])
+            if q > 0:
+                block_order.append((q - 1, N_GATES - 1))
+        block_order.append((PAIRS - 1, N_GATES - 1))
+        groups = [(q * PAIR + t, g) for q, g in block_order for t in range(PAIR)]
+        first_of_last = groups.index(((PAIRS - 1) * PAIR, 0))
+        groups[first_of_last : first_of_last + PAIR * (N_GATES - 1)] = [
+            ((PAIRS - 1) * PAIR + t, g) for t in range(PAIR) for g in range(N_GATES - 1)
+        ]
+
+        later = {}
+
+        def at_slot(s, call):
+            later.setdefault(s, []).append(call)
+
+        def finish_gate(s, b, g):
+            activate(b, g)
+            last_pair = b // PAIR == PAIRS - 1
+            last_tile = b == TILES - 1
+            if g == 1:
+                if last_tile:
+                    at_slot(s + 1, lambda: f_times_c(nc.vector, b))
+                else:
+                    f_times_c(nc.gpsimd, b)
+            elif g == 2:
+                if last_tile:
+                    at_slot(s + 1, lambda: i_times_g(nc.vector, b))
+                    at_slot(s + 2, lambda: c_sum(nc.vector, b))
+                    at_slot(s + 2, lambda: tanh_c_new(b))
+                else:
+                    i_times_g(nc.gpsimd, b)
+                    c_sum(nc.gpsimd, b)
+                    at_slot(s + (3 if last_pair else 4), lambda: tanh_c_new(b))
+            elif g == 3:
+                if last_pair:
+                    at_slot(s + 1, lambda: h_product(nc.vector, b))
+                    at_slot(s + 1, lambda: h_store(b - 1))
+                elif b // PAIR == PAIRS - 2:
+                    h_product(nc.gpsimd, b, store_now=False)
+                    if b % PAIR == 0:
+                        at_slot(s + 1, lambda: h_store(b))
+                elif b < 2 * PAIR:
+                    at_slot(s + 1, lambda: h_product(nc.vector, b))
+                else:
+                    h_product(nc.gpsimd, b)
+
+        half = FEAT // 2
+        pl_0 = psum.tile([P, FEAT], F32, tag="bank")
+        pl_1 = psum.tile([P, FEAT], F32, tag="bank")
+        f_ps_0 = psum.tile([P, WORD_CHUNKS, PAIR, P], F32, tag="bank")
+        plain_matmuls(pl_0[:, :half], 0, 0, 0, half, flip_transposes(f_ps_0, w_flip(2)))
+        flip_copy(f_ps_0, w_flip(2))
+        x_ps = psum.tile([P, PAIR, 2, P], F32, tag="bank")
+        plain_matmuls(pl_1[:, :half], 1, 0, 0, half, x_transposes(x_ps, 0))
+        x_copy(x_ps, 0)
+        f_ps_1 = psum.tile([P, WORD_CHUNKS, PAIR, P], F32, tag="bank")
+        plain_matmuls(pl_0[:, half:], 0, 0, half, FEAT, flip_transposes(f_ps_1, w_flip(3)))
+        flip_copy(f_ps_1, w_flip(3))
+        plain_matmuls(pl_1[:, half:], 1, 0, half, FEAT, [])
+        spread_biases(3, nc.scalar.copy)
+        x_quantise(0)
+        mx_done = 2 * PAIR
+        fetch(pl_0, 0, 0)
+        fetch(pl_1, 1, 0)
+        passes = [(mx_pass(mb, mg), mb, mg) for mb, mg in groups[:mx_done]]
+        for mx_ps, mb, mg in passes:
+            if fetch(mx_ps, mb, mg):
+                finish_gate(1, mb, mg)
+
+        for s, (b, g) in enumerate(groups):
+            if s < PAIR or s == GROUPS - 1:
+                continue
+            q, t = divmod(b, PAIR)
+            if q == 0 and g == 1:
+                flips = [w_flip((g + 1) * (ROW_TILES // PAIR) + t)]
+            elif q == 1 and g == 0:
+                flips = [w_flip(3 * (ROW_TILES // PAIR) + t)]
+            elif g == 2 and t == 0 and q + 1 < PAIRS:
+                flips = [h_flip(q + 1)]
+            else:
+                flips = []
+            if s == PAIR:
+                x_pair = 1
+            elif g == 2 and t == 1 and q + 2 < PAIRS:
+                x_pair = q + 2
+            else:
+                x_pair = 0
+            banks = []
+            riders = []
+            for flip in flips:
+                flip_ps = psum.tile([P, WORD_CHUNKS, PAIR, P], F32, tag="bank")
+                banks.append(flip_ps)
+                riders.extend(flip_transposes(flip_ps, flip))
+            if x_pair:
+                x_ps = psum.tile([P, PAIR, 2, P], F32, tag="bank")
+                riders.extend(x_transposes(x_ps, x_pair))
+            pl_ps = plain_group(b, g, riders)
+            for flip, flip_ps in zip(flips, banks):
+                flip_copy(flip_ps, flip)
+            if x_pair:
+                x_copy(x_ps, x_pair)
+            mx_wanted = min(GROUPS, s + 1 + min(s + 1, MX_LEAD))
+            passes = [(mx_pass(mb, mg), mb, mg) for mb, mg in groups[mx_done:mx_wanted]]
+            mx_done = mx_wanted
+            if fetch(pl_ps, b, g):
+                finish_gate(s, b, g)
+            for mx_ps, mb, mg in passes:
+                if fetch(mx_ps, mb, mg):
+                    finish_gate(s, mb, mg)
+            if x_pair:
+                x_quantise(x_pair)
+            for call in later.get(s, []):
+                call()
+
+        b, g = groups[GROUPS - 1]
+        end_0 = psum.tile([P, half], F32, tag="bank")
+        end_1 = psum.tile([P, half], F32, tag="bank")
+        for end_ps, lo in ((end_0, 0), (end_1, half)):
+            plain_matmuls(end_ps[:], b, g, lo, lo + half, [])
+        for end_ps, lo in ((end_0, 0), (end_1, half)):
+            fetch(end_ps, b, g, lo, lo + half)
+            activate(b, g, lo, lo + half)
+        for call in later.get(GROUPS - 1, []):
+            call()
+        for lo in (0, half):
+            h_product(nc.vector, b, lo, lo + half)

@@ -76,11 +76,11 @@ def tile_int8lstmcell_kernel(
         def gate(b, g, lo=0, hi=FEAT):
             return gates[:, b, g * FEAT + lo : g * FEAT + hi]
 
+        nc.gpsimd.memset(bias_rows[:].bitcast(I32), 0)
         nc.vector.memset(ones[:], 1.0)
-        nc.gpsimd.memset(zeros[:], 0.0)
-        nc.vector.memset(bias_rows[:].bitcast(I32), 0)
-        nc.vector.memset(w_plane[:].bitcast(I32), 0)
+        nc.vector.memset(zeros[:], 0.0)
         nc.vector.memset(warm[:], 0.0)
+        nc.vector.memset(w_plane[:].bitcast(I32), 0)
         make_identity(nc, ident_f32[:])
         nc.scalar.activation(out=warm[:], in_=warm[:], func=SIGMOID)
 
@@ -98,9 +98,9 @@ def tile_int8lstmcell_kernel(
             )
 
         load_pair(h_sb, h_view, 0)
+        load_w_hh(0)
         nc.sync.dma_start(out=bias_rows[0:1, :], in_=bias_ih.rearrange("(o n) -> o n", o=1))
         nc.sync.dma_start(out=bias_rows[1:2, :], in_=bias_hh.rearrange("(o n) -> o n", o=1))
-        load_w_hh(0)
         load_w_hh(1)
         load_w_hh(2)
         load_pair(x_sb, x_view, 0)
@@ -249,11 +249,11 @@ def tile_int8lstmcell_kernel(
         for i in range(WARM_UPS):
             nc.tensor.matmul(out=warm_ps[:], lhsT=ones[:], rhs=zeros[:], start=True, stop=True)
         flip_now(h_flip(0))
-        spread_biases(0, nc.vector.tensor_copy)
         flip_now(w_flip(0))
-        spread_biases(1, nc.vector.tensor_copy)
+        spread_biases(0, nc.vector.tensor_copy)
         flip_now(w_flip(1))
-        spread_biases(2, nc.vector.tensor_copy)
+        for g in range(1, N_GATES):
+            spread_biases(g, nc.vector.tensor_copy)
 
         block_order = []
         for q in range(PAIRS):
@@ -262,10 +262,7 @@ def tile_int8lstmcell_kernel(
                 block_order.append((q - 1, N_GATES - 1))
         block_order.append((PAIRS - 1, N_GATES - 1))
         groups = [(q * PAIR + t, g) for q, g in block_order for t in range(PAIR)]
-        first_of_last = groups.index(((PAIRS - 1) * PAIR, 0))
-        groups[first_of_last : first_of_last + PAIR * (N_GATES - 1)] = [
-            ((PAIRS - 1) * PAIR + t, g) for t in range(PAIR) for g in range(N_GATES - 1)
-        ]
+        groups[groups.index(((PAIRS - 1) * PAIR, 0)) :] = [(6,0),(6,1),(6,2),(7,0),(7,1),(7,2),(4,3),(5,3),(6,3),(7,3)]
 
         later = {}
 
@@ -283,7 +280,7 @@ def tile_int8lstmcell_kernel(
                     f_times_c(nc.gpsimd, b)
             elif g == 2:
                 if last_tile:
-                    at_slot(s + 1, lambda: i_times_g(nc.vector, b))
+                    i_times_g(nc.gpsimd, b)
                     at_slot(s + 2, lambda: c_sum(nc.vector, b))
                     at_slot(s + 2, lambda: tanh_c_new(b))
                 else:
@@ -293,11 +290,9 @@ def tile_int8lstmcell_kernel(
             elif g == 3:
                 if last_pair:
                     at_slot(s + 1, lambda: h_product(nc.vector, b))
-                    at_slot(s + 1, lambda: h_store(b - 1))
                 elif b // PAIR == PAIRS - 2:
                     h_product(nc.gpsimd, b, store_now=False)
-                    if b % PAIR == 0:
-                        at_slot(s + 1, lambda: h_store(b))
+                    at_slot(min(s + 1, GROUPS - 1), lambda: h_store(b))
                 elif b < 2 * PAIR:
                     at_slot(s + 1, lambda: h_product(nc.vector, b))
                 else:
@@ -316,7 +311,6 @@ def tile_int8lstmcell_kernel(
         plain_matmuls(pl_0[:, half:], 0, 0, half, FEAT, flip_transposes(f_ps_1, w_flip(3)))
         flip_copy(f_ps_1, w_flip(3))
         plain_matmuls(pl_1[:, half:], 1, 0, half, FEAT, [])
-        spread_biases(3, nc.scalar.copy)
         x_quantise(0)
         mx_done = 2 * PAIR
         fetch(pl_0, 0, 0)
@@ -363,11 +357,11 @@ def tile_int8lstmcell_kernel(
             mx_done = mx_wanted
             if fetch(pl_ps, b, g):
                 finish_gate(s, b, g)
+            if x_pair:
+                x_quantise(x_pair)
             for mx_ps, mb, mg in passes:
                 if fetch(mx_ps, mb, mg):
                     finish_gate(s, mb, mg)
-            if x_pair:
-                x_quantise(x_pair)
             for call in later.get(s, []):
                 call()
 

@@ -62,6 +62,7 @@ def tile_int8lstmcell_kernel(
         zeros = keep.tile([P, FEAT], BF16)
         ident_f32 = keep.tile([P, P], F32)
         warm = keep.tile([P, 1], F32)
+        x_sorted = keep.tile([P, PAIR, 2, P], F32)
         x_grouped = keep.tile([P, BATCH * 4], BF16, align_bytes=64)
         x_codes = keep.tile([P, BATCH], U32, align_bytes=64)
         x_plane = keep.tile([P, BATCH], U8, align_bytes=64)
@@ -116,21 +117,27 @@ def tile_int8lstmcell_kernel(
         load_pair(x_sb, x_view, 1)
         load_w_hh(5)
         load_words(2)
+        load_pair(x_sb, x_view, 2)
+        load_pair(c_sb, c_view, 0)
+        load_pair(h_sb, h_view, 1)
         load_w_hh(6)
         load_w_hh(7)
         load_words(3)
-        for q in range(PAIRS):
+        load_pair(x_sb, x_view, 3)
+        for q in range(1, PAIRS):
             load_pair(c_sb, c_view, q)
             if q + 1 < PAIRS:
                 load_pair(h_sb, h_view, q + 1)
-            if q + 2 < PAIRS:
-                load_pair(x_sb, x_view, q + 2)
 
         grouped_words = x_grouped[:].bitcast(F32).rearrange("p (b r u) -> p b r u", b=TILES, u=2)
 
         def x_transposes(x_ps, q):
             return [
-                (x_ps[:, t, u, :], x_sb[:, q * PAIR + t, :].bitcast(F32)[:, u : FEAT // 2 : 2], ident_f32[:])
+                (
+                    x_ps[:, t, u, :],
+                    x_sorted[:, t, u, :] if q == 0 else x_sb[:, q * PAIR + t, :].bitcast(F32)[:, u : FEAT // 2 : 2],
+                    ident_f32[:],
+                )
                 for t in range(PAIR)
                 for u in range(2)
             ]
@@ -252,8 +259,14 @@ def tile_int8lstmcell_kernel(
         flip_now(w_flip(0))
         spread_biases(0, nc.vector.tensor_copy)
         flip_now(w_flip(1))
-        for g in range(1, N_GATES):
-            spread_biases(g, nc.vector.tensor_copy)
+        spread_biases(1, nc.vector.tensor_copy)
+        for t in range(PAIR):
+            nc.vector.tensor_copy(
+                out=x_sorted[:, t, :, :], in_=x_sb[:, t, :].bitcast(F32).rearrange("p (w u) -> p u w", u=2)
+            )
+
+        spread_biases(2, nc.vector.tensor_copy)
+        spread_biases(3, nc.vector.tensor_copy)
 
         block_order = []
         for q in range(PAIRS):
@@ -293,7 +306,7 @@ def tile_int8lstmcell_kernel(
                 elif b // PAIR == PAIRS - 2:
                     h_product(nc.gpsimd, b, store_now=False)
                     at_slot(min(s + 1, GROUPS - 1), lambda: h_store(b))
-                elif b < 2 * PAIR:
+                elif b % PAIR == 0 and b < 2 * PAIR:
                     at_slot(s + 1, lambda: h_product(nc.vector, b))
                 else:
                     h_product(nc.gpsimd, b)

@@ -197,7 +197,7 @@ def tile_int8lstmcell_kernel(
             nc.scalar.copy(out=flip[1], in_=flip_ps[:].rearrange("p j i r -> p j (i r)"))
 
         def plain_matmuls(sums, b, g, lo, hi, riders):
-            share = -(-len(riders) // (K_CHUNKS - 1))
+            share = -(-len(riders) // (K_CHUNKS - 2))
             for kc in range(K_CHUNKS):
                 nc.tensor.matmul(
                     out=sums,
@@ -206,9 +206,8 @@ def tile_int8lstmcell_kernel(
                     start=(kc == 0),
                     stop=(kc == K_CHUNKS - 1),
                 )
-                if kc > 0 or len(riders) > 2 * share:
-                    first = (kc - 1 if len(riders) <= 2 * share else kc) * share
-                    for out, in_, identity in riders[first : first + share]:
+                if kc > 0:
+                    for out, in_, identity in riders[(kc - 1) * share : kc * share]:
                         nc.tensor.transpose(out, in_, identity)
 
         def plain_group(b, g, riders):
@@ -258,8 +257,8 @@ def tile_int8lstmcell_kernel(
         flip_now(h_flip(0))
         flip_now(w_flip(0))
         spread_biases(0, nc.vector.tensor_copy)
-        flip_now(w_flip(1))
         spread_biases(1, nc.vector.tensor_copy)
+        flip_now(w_flip(1))
         for t in range(PAIR):
             nc.vector.tensor_copy(
                 out=x_sorted[:, t, :, :], in_=x_sb[:, t, :].bitcast(F32).rearrange("p (w u) -> p u w", u=2)

from contextlib import ExitStack

import concourse.mybir as mybir
from concourse.masks import make_identity

BF16 = mybir.dt.bfloat16
F32 = mybir.dt.float32
I32 = mybir.dt.int32
U32 = mybir.dt.uint32
U8 = mybir.dt.uint8
FP8X4 = mybir.dt.float8_e4m3fn_x4
ADD = mybir.AluOpType.add
MULT = mybir.AluOpType.mult
SIGMOID = mybir.ActivationFunctionType.Sigmoid
TANH = mybir.ActivationFunctionType.Tanh

P = 128
BATCH = 1024
FEAT = 512
N_GATES = 4
GATE_COLS = N_GATES * FEAT
TILES = BATCH // P
K_CHUNKS = FEAT // P
WORD_CHUNKS = FEAT // 2 // P
PAIR = 2
PAIRS = TILES // PAIR
ROW_TILES = FEAT // P
BLOCKS = PAIRS * N_GATES
GROUPS = BLOCKS * PAIR
WARM_UPS = 4
MX_LEAD = 8

FLOPS = 2 * BATCH * FEAT * GATE_COLS * 2


def tile_int8lstmcell_kernel(
    tc, x, h_prev, c_prev, w_ih_words, w_ih_scales, w_hh, bias_ih, bias_hh, out_0, out_1
):
    nc = tc.nc
    with ExitStack() as stack:
        keep = stack.enter_context(tc.tile_pool(name="keep", bufs=1))
        psum = stack.enter_context(tc.psum_pool(name="psum", bufs=8))
        stack.enter_context(tc.manual_schedule())

        x_view = x.rearrange("(p b) k -> p b k", b=TILES)
        h_view = h_prev.rearrange("(p b) k -> p b k", b=TILES)
        c_view = c_prev.rearrange("(p b) k -> p b k", b=TILES)
        h_new_view = out_0.rearrange("(p b) n -> p b n", b=TILES)
        c_new_view = out_1.rearrange("(p b) n -> p b n", b=TILES)
        w_hh_view = w_hh.rearrange("(j p) k -> p j k", p=P)
        words_view = w_ih_words[0].rearrange("p n t -> p (n t)")

        x_sb = keep.tile([P, TILES, FEAT], BF16)
        h_sb = keep.tile([P, TILES, FEAT], BF16)
        c_sb = keep.tile([P, TILES, FEAT], BF16)
        w_sb = keep.tile([P, N_GATES * ROW_TILES, FEAT], BF16)
        w_words = keep.tile([P, GATE_COLS], U32, align_bytes=64)
        w_plane = keep.tile([P, GATE_COLS], U8, align_bytes=64)
        bias_rows = keep.tile([P, GATE_COLS], BF16)
        bias_all = keep.tile([P, GATE_COLS], F32)
        ones = keep.tile([P, P], BF16)
        zeros = keep.tile([P, FEAT], BF16)
        ident_f32 = keep.tile([P, P], F32)
        warm = keep.tile([P, 1], F32)
        x_sorted = keep.tile([P, PAIR, 2, P], F32)
        x_grouped = keep.tile([P, BATCH * 4], BF16, align_bytes=64)
        x_codes = keep.tile([P, BATCH], U32, align_bytes=64)
        x_plane = keep.tile([P, BATCH], U8, align_bytes=64)
        h_t = keep.tile([P, WORD_CHUNKS, BATCH], F32)
        w_t = keep.tile([P, WORD_CHUNKS, GATE_COLS], F32)
        h_t_halves = h_t[:].rearrange("p j r -> p (j r)").bitcast(BF16).rearrange("p (j r e) -> p j r e", j=WORD_CHUNKS, e=2)
        w_t_halves = w_t[:].rearrange("p j r -> p (j r)").bitcast(BF16).rearrange("p (j r e) -> p j r e", j=WORD_CHUNKS, e=2)
        gates = keep.tile([P, TILES, GATE_COLS], F32)
        c_new = keep.tile([P, TILES, FEAT], F32)
        h_new = keep.tile([P, TILES, FEAT], F32)

        def gate(b, g, lo=0, hi=FEAT):
            return gates[:, b, g * FEAT + lo : g * FEAT + hi]

        nc.gpsimd.memset(bias_rows[:].bitcast(I32), 0)
        nc.vector.memset(ones[:], 1.0)
        nc.vector.memset(zeros[:], 0.0)
        nc.vector.memset(warm[:], 0.0)
        nc.vector.memset(w_plane[:].bitcast(I32), 0)
        make_identity(nc, ident_f32[:])
        nc.scalar.activation(out=warm[:], in_=warm[:], func=SIGMOID)

        def load_pair(dst, src, q):
            nc.sync.dma_start(out=dst[:, q * PAIR : (q + 1) * PAIR, :], in_=src[:, q * PAIR : (q + 1) * PAIR, :])

        def load_w_hh(jj):
            row_tiles = slice(jj * PAIR, (jj + 1) * PAIR)
            nc.sync.dma_start(out=w_sb[:, row_tiles, :], in_=w_hh_view[:, row_tiles, :])

        def load_words(g):
            nc.sync.dma_start(
                out=w_words[:, g * FEAT : (g + 1) * FEAT].bitcast(I32),
                in_=words_view[:, g * FEAT * 4 : (g + 1) * FEAT * 4].bitcast(I32),
            )

        load_pair(h_sb, h_view, 0)
        load_w_hh(0)
        nc.sync.dma_start(out=bias_rows[0:1, :], in_=bias_ih.rearrange("(o n) -> o n", o=1))
        nc.sync.dma_start(out=bias_rows[1:2, :], in_=bias_hh.rearrange("(o n) -> o n", o=1))
        load_w_hh(1)
        load_w_hh(2)
        load_pair(x_sb, x_view, 0)
        load_w_hh(3)
        for s in range(4):
            nc.sync.dma_start(
                out=w_plane[32 * s : 32 * s + 4, :].bitcast(I32),
                in_=w_ih_scales[0, 4 * s : 4 * s + 4, :].bitcast(I32),
            )
        load_words(0)
        load_words(1)
        load_w_hh(4)
        load_pair(x_sb, x_view, 1)
        load_w_hh(5)
        load_words(2)
        load_pair(x_sb, x_view, 2)
        load_pair(c_sb, c_view, 0)
        load_pair(h_sb, h_view, 1)
        load_w_hh(6)
        load_w_hh(7)
        load_words(3)
        load_pair(x_sb, x_view, 3)
        for q in range(1, PAIRS):
            load_pair(c_sb, c_view, q)
            if q + 1 < PAIRS:
                load_pair(h_sb, h_view, q + 1)

        grouped_words = x_grouped[:].bitcast(F32).rearrange("p (b r u) -> p b r u", b=TILES, u=2)

        def x_transposes(x_ps, q):
            return [
                (
                    x_ps[:, t, u, :],
                    x_sorted[:, t, u, :] if q == 0 else x_sb[:, q * PAIR + t, :].bitcast(F32)[:, u : FEAT // 2 : 2],
                    ident_f32[:],
                )
                for t in range(PAIR)
                for u in range(2)
            ]

        def x_copy(x_ps, q):
            nc.scalar.copy(
                out=grouped_words[:, q * PAIR : (q + 1) * PAIR, :, :], in_=x_ps[:].rearrange("p t u r -> p t r u")
            )

        def x_quantise(q):
            rows = slice(q * PAIR * P, (q + 1) * PAIR * P)
            nc.vector.quantize_mx(
                out=x_codes[:, rows].bitcast(FP8X4),
                scales=x_plane[:, rows],
                in_=x_grouped[:, q * PAIR * P * 4 : (q + 1) * PAIR * P * 4],
            )

        def mx_pass(b, g):
            rows = slice(b * P, (b + 1) * P)
            cols = slice(g * FEAT, (g + 1) * FEAT)
            mx_ps = psum.tile([P, FEAT], F32, tag="bank")
            nc.tensor.matmul_mx(
                out=mx_ps[:],
                lhsT=x_codes[:, rows].bitcast(FP8X4),
                lhsT_scale=x_plane[:, rows],
                rhs=w_words[:, cols].bitcast(FP8X4),
                rhs_scale=w_plane[:, cols],
                start=True,
                stop=True,
            )
            return mx_ps

        begun = set()

        def fetch(sums_ps, b, g, lo=0, hi=FEAT):
            complete = (b, g) in begun
            other = gate(b, g, lo, hi) if complete else bias_all[:, g * FEAT + lo : g * FEAT + hi]
            nc.vector.tensor_tensor(out=gate(b, g, lo, hi), in0=sums_ps[:], in1=other, op=ADD)
            if hi == FEAT:
                begun.add((b, g))
            return complete

        def w_flip(jj):
            return ([w_sb[:, jj * PAIR + i, :] for i in range(PAIR)], w_t[:, :, jj * PAIR * P : (jj + 1) * PAIR * P])

        def h_flip(q):
            return ([h_sb[:, q * PAIR + i, :] for i in range(PAIR)], h_t[:, :, q * PAIR * P : (q + 1) * PAIR * P])

        def flip_transposes(flip_ps, flip):
            return [
                (flip_ps[:, j, i, :], flip[0][i].bitcast(F32)[:, j * P : (j + 1) * P], ident_f32[:])
                for i in range(PAIR)
                for j in range(WORD_CHUNKS)
            ]

        def flip_copy(flip_ps, flip):
            nc.scalar.copy(out=flip[1], in_=flip_ps[:].rearrange("p j i r -> p j (i r)"))

        def plain_matmuls(sums, b, g, lo, hi, riders):
            share = -(-len(riders) // (K_CHUNKS - 2))
            for kc in range(K_CHUNKS):
                nc.tensor.matmul(
                    out=sums,
                    lhsT=h_t_halves[:, kc // 2, b * P : (b + 1) * P, kc % 2],
                    rhs=w_t_halves[:, kc // 2, g * FEAT + lo : g * FEAT + hi, kc % 2],
                    start=(kc == 0),
                    stop=(kc == K_CHUNKS - 1),
                )
                if kc > 0:
                    for out, in_, identity in riders[(kc - 1) * share : kc * share]:
                        nc.tensor.transpose(out, in_, identity)

        def plain_group(b, g, riders):
            pl_ps = psum.tile([P, FEAT], F32, tag="bank")
            plain_matmuls(pl_ps[:], b, g, 0, FEAT, riders)
            return pl_ps

        def activate(b, g, lo=0, hi=FEAT):
            nc.scalar.activation(out=gate(b, g, lo, hi), in_=gate(b, g, lo, hi), func=(TANH if g == 2 else SIGMOID))

        def f_times_c(cell, b):
            cell.tensor_tensor(out=gate(b, 1), in0=gate(b, 1), in1=c_sb[:, b, :], op=MULT)

        def i_times_g(cell, b):
            cell.tensor_tensor(out=gate(b, 0), in0=gate(b, 0), in1=gate(b, 2), op=MULT)

        def c_sum(cell, b):
            cell.tensor_tensor(out=c_new[:, b, :], in0=gate(b, 1), in1=gate(b, 0), op=ADD)
            nc.sync.dma_start(out=c_new_view[:, b, :], in_=c_new[:, b, :])

        def tanh_c_new(b):
            nc.scalar.activation(out=gate(b, 2), in_=c_new[:, b, :], func=TANH)

        def h_store(b, lo=0, hi=FEAT):
            nc.sync.dma_start(out=h_new_view[:, b, lo:hi], in_=h_new[:, b, lo:hi])

        def h_product(cell, b, lo=0, hi=FEAT, store_now=True):
            cell.tensor_tensor(out=h_new[:, b, lo:hi], in0=gate(b, 3, lo, hi), in1=gate(b, 2, lo, hi), op=MULT)
            if store_now:
                h_store(b, lo, hi)

        def flip_now(flip):
            flip_ps = psum.tile([P, WORD_CHUNKS, PAIR, P], F32, tag="bank")
            for out, in_, identity in flip_transposes(flip_ps, flip):
                nc.tensor.transpose(out, in_, identity)
            flip_copy(flip_ps, flip)

        def spread_biases(g, copy):
            cols = slice(g * FEAT, (g + 1) * FEAT)
            bias_ps = psum.tile([P, FEAT], F32, tag="bank")
            nc.tensor.matmul(out=bias_ps[:], lhsT=ones[:], rhs=bias_rows[:, cols], start=True, stop=True)
            copy(out=bias_all[:, cols], in_=bias_ps[:])

        warm_ps = psum.tile([P, FEAT], F32, tag="bank")
        for i in range(WARM_UPS):
            nc.tensor.matmul(out=warm_ps[:], lhsT=ones[:], rhs=zeros[:], start=True, stop=True)
        flip_now(h_flip(0))
        flip_now(w_flip(0))
        spread_biases(0, nc.vector.tensor_copy)
        spread_biases(1, nc.vector.tensor_copy)
        flip_now(w_flip(1))
        for t in range(PAIR):
            nc.vector.tensor_copy(
                out=x_sorted[:, t, :, :], in_=x_sb[:, t, :].bitcast(F32).rearrange("p (w u) -> p u w", u=2)
            )

        spread_biases(2, nc.vector.tensor_copy)
        spread_biases(3, nc.vector.tensor_copy)

        block_order = []
        for q in range(PAIRS):
            block_order.extend([(q, g) for g in range(N_GATES - 1)])
            if q > 0:
                block_order.append((q - 1, N_GATES - 1))
        block_order.append((PAIRS - 1, N_GATES - 1))
        groups = [(q * PAIR + t, g) for q, g in block_order for t in range(PAIR)]
        groups[groups.index(((PAIRS - 1) * PAIR, 0)) :] = [(6,0),(6,1),(6,2),(7,0),(7,1),(7,2),(4,3),(5,3),(6,3),(7,3)]

        later = {}

        def at_slot(s, call):
            later.setdefault(s, []).append(call)

        def finish_gate(s, b, g):
            activate(b, g)
            last_pair = b // PAIR == PAIRS - 1
            last_tile = b == TILES - 1
            if g == 1:
                if last_tile:
                    at_slot(s + 1, lambda: f_times_c(nc.vector, b))
                else:
                    f_times_c(nc.gpsimd, b)
            elif g == 2:
                if last_tile:
                    i_times_g(nc.gpsimd, b)
                    at_slot(s + 2, lambda: c_sum(nc.vector, b))
                    at_slot(s + 2, lambda: tanh_c_new(b))
                else:
                    i_times_g(nc.gpsimd, b)
                    c_sum(nc.gpsimd, b)
                    at_slot(s + (3 if last_pair else 4), lambda: tanh_c_new(b))
            elif g == 3:
                if last_pair:
                    at_slot(s + 1, lambda: h_product(nc.vector, b))
                elif b // PAIR == PAIRS - 2:
                    h_product(nc.gpsimd, b, store_now=False)
                    at_slot(min(s + 1, GROUPS - 1), lambda: h_store(b))
                elif b % PAIR == 0 and b < 2 * PAIR:
                    at_slot(s + 1, lambda: h_product(nc.vector, b))
                else:
                    h_product(nc.gpsimd, b)

        half = FEAT // 2
        pl_0 = psum.tile([P, FEAT], F32, tag="bank")
        pl_1 = psum.tile([P, FEAT], F32, tag="bank")
        f_ps_0 = psum.tile([P, WORD_CHUNKS, PAIR, P], F32, tag="bank")
        plain_matmuls(pl_0[:, :half], 0, 0, 0, half, flip_transposes(f_ps_0, w_flip(2)))
        flip_copy(f_ps_0, w_flip(2))
        x_ps = psum.tile([P, PAIR, 2, P], F32, tag="bank")
        plain_matmuls(pl_1[:, :half], 1, 0, 0, half, x_transposes(x_ps, 0))
        x_copy(x_ps, 0)
        f_ps_1 = psum.tile([P, WORD_CHUNKS, PAIR, P], F32, tag="bank")
        plain_matmuls(pl_0[:, half:], 0, 0, half, FEAT, flip_transposes(f_ps_1, w_flip(3)))
        flip_copy(f_ps_1, w_flip(3))
        plain_matmuls(pl_1[:, half:], 1, 0, half, FEAT, [])
        x_quantise(0)
        mx_done = 2 * PAIR
        fetch(pl_0, 0, 0)
        fetch(pl_1, 1, 0)
        passes = [(mx_pass(mb, mg), mb, mg) for mb, mg in groups[:mx_done]]
        for mx_ps, mb, mg in passes:
            if fetch(mx_ps, mb, mg):
                finish_gate(1, mb, mg)

        for s, (b, g) in enumerate(groups):
            if s < PAIR or s == GROUPS - 1:
                continue
            q, t = divmod(b, PAIR)
            if q == 0 and g == 1:
                flips = [w_flip((g + 1) * (ROW_TILES // PAIR) + t)]
            elif q == 1 and g == 0:
                flips = [w_flip(3 * (ROW_TILES // PAIR) + t)]
            elif g == 2 and t == 0 and q + 1 < PAIRS:
                flips = [h_flip(q + 1)]
            else:
                flips = []
            if s == PAIR:
                x_pair = 1
            elif g == 2 and t == 1 and q + 2 < PAIRS:
                x_pair = q + 2
            else:
                x_pair = 0
            banks = []
            riders = []
            for flip in flips:
                flip_ps = psum.tile([P, WORD_CHUNKS, PAIR, P], F32, tag="bank")
                banks.append(flip_ps)
                riders.extend(flip_transposes(flip_ps, flip))
            if x_pair:
                x_ps = psum.tile([P, PAIR, 2, P], F32, tag="bank")
                riders.extend(x_transposes(x_ps, x_pair))
            pl_ps = plain_group(b, g, riders)
            for flip, flip_ps in zip(flips, banks):
                flip_copy(flip_ps, flip)
            if x_pair:
                x_copy(x_ps, x_pair)
            mx_wanted = min(GROUPS, s + 1 + min(s + 1, MX_LEAD))
            passes = [(mx_pass(mb, mg), mb, mg) for mb, mg in groups[mx_done:mx_wanted]]
            mx_done = mx_wanted
            if fetch(pl_ps, b, g):
                finish_gate(s, b, g)
            if x_pair:
                x_quantise(x_pair)
            for mx_ps, mb, mg in passes:
                if fetch(mx_ps, mb, mg):
                    finish_gate(s, mb, mg)
            for call in later.get(s, []):
                call()

        b, g = groups[GROUPS - 1]
        end_0 = psum.tile([P, half], F32, tag="bank")
        end_1 = psum.tile([P, half], F32, tag="bank")
        for end_ps, lo in ((end_0, 0), (end_1, half)):
            plain_matmuls(end_ps[:], b, g, lo, lo + half, [])
        for end_ps, lo in ((end_0, 0), (end_1, half)):
            fetch(end_ps, b, g, lo, lo + half)
            activate(b, g, lo, lo + half)
        for call in later.get(GROUPS - 1, []):
            call()
        for lo in (0, half):
            h_product(nc.vector, b, lo, lo + half)
